import numpy as np
import ml_dtypes


def mxq(x, axis, fmt="e4m3"):
    dtype, down = {"e4m3": (ml_dtypes.float8_e4m3fn, 7), "e5m2": (ml_dtypes.float8_e5m2, 14)}[fmt]
    v = np.moveaxis(np.asarray(x, np.float32).astype(ml_dtypes.bfloat16).astype(np.float64), axis, -1)
    blocks = v.reshape(v.shape[:-1] + (-1, 32))
    amax = np.abs(blocks).max(-1, keepdims=True)
    byte = np.maximum(np.where(amax > 0, np.frexp(amax)[1] - 1 + 127, 0) - down, 1)
    scale = np.exp2(byte - 127.0)
    codes = (blocks / scale).astype(np.float32).astype(dtype).astype(np.float64)
    return np.moveaxis((codes * scale).reshape(v.shape), -1, axis)


WIDE = False


def mx_kscale(k):
    if not WIDE:
        return np.ones(k)
    levels = np.array([10, -10, 5, -5, 0])
    a = np.random.permutation(np.resize(levels, k // 512 * 4)).reshape(k // 512, 4)
    idx = np.arange(k)
    return np.exp2(a[idx // 512, idx % 128 // 32])


BF16 = ml_dtypes.bfloat16


def bf(x):
    return np.asarray(x, np.float32).astype(BF16)


def f64(x):
    return np.asarray(x).astype(np.float64)


E2M1 = np.array([0.0, 0.5, 1.0, 1.5, 2.0, 3.0, 4.0, 6.0, -0.0, -0.5, -1.0, -1.5, -2.0, -3.0, -4.0, -6.0])


def pack_weight(w, fmt):
    k, n = w.shape
    w = f64(bf(w)).reshape(k // 32, 32, n)
    amax = np.abs(w).max(1)
    if fmt == "e4m3":
        byte = np.frexp(amax)[1] - 1 + 127 - 7
    else:
        mant, ex = np.frexp(amax / 6.0)
        byte = np.where(mant > 0.5, ex, ex - 1) + 127
    byte = np.clip(np.where(amax > 0, byte, 1), 1, 254)
    scaled = (w * np.exp2(127.0 - byte)[:, None, :]).reshape(k, n).astype(np.float32)
    by_word = np.ascontiguousarray(scaled.reshape(k // 512, 128, 4, n).transpose(0, 1, 3, 2))
    if fmt == "e4m3":
        words = by_word.astype(ml_dtypes.float8_e4m3fn).view(np.uint8)
    else:
        c = by_word.astype(ml_dtypes.float4_e2m1fn).view(np.uint8) & 0xF
        words = c[..., 0::2] | (c[..., 1::2] << 4)
    return np.ascontiguousarray(words), np.ascontiguousarray(byte.astype(np.uint8).reshape(k // 512, 16, n))


def unpack_weight(words, scales, fmt):
    g, p, n, _ = words.shape
    if fmt == "e4m3":
        vals = np.ascontiguousarray(words).view(ml_dtypes.float8_e4m3fn).astype(np.float64)
    else:
        nib = np.empty((g, p, n, 4), np.uint8)
        nib[..., 0::2] = words & 0xF
        nib[..., 1::2] = words >> 4
        vals = E2M1[nib]
    vals = vals * np.repeat(np.exp2(scales.astype(np.float64) - 127.0), 8, axis=1)[..., None]
    return vals.transpose(0, 1, 3, 2).reshape(g * 512, n)


BS, N, Bb, Cc, D, H, DP = 2, 128, 2, 2, 512, 2048, 512
G = Bb * Cc
P = 4 * D
FMT = "e4m3"


def gmm(x, w):
    return (mxq(x, 3, "e4m3").transpose(0, 2, 1, 3) @ w).transpose(0, 2, 1, 3)


def unit_normalize(x):
    return x / np.maximum(np.sqrt((x * x).sum(-1, keepdims=True)), 1e-6)


def setup_inputs():
    s = mx_kscale(H)
    rn = np.random.standard_normal
    a = rn((BS, N, G, H))
    ffn_act = bf(a / (1.0 + np.exp(-1.702 * a)) * s)
    x_mix = bf(rn((BS, N, G, D)))
    down_w = rn((G, H, D)) / np.sqrt(H) / s[:, None]
    down_b = bf(0.1 * rn((G, D)))
    post_w = rn((G, D, P)) / np.sqrt(D)
    post_b = bf(0.1 * rn((G, P)))
    down_w_words, down_w_scales = pack_weight(down_w.reshape(-1, D), FMT)
    post_w_words, post_w_scales = pack_weight(post_w.reshape(-1, P), FMT)
    return {
        "ffn_act": ffn_act,
        "x_mix": x_mix,
        "down_w_words": down_w_words,
        "down_w_scales": down_w_scales,
        "down_b": down_b,
        "post_w_words": post_w_words,
        "post_w_scales": post_w_scales,
        "post_b": post_b,
    }


def reference(ffn_act, x_mix, down_w_words, down_w_scales, down_b, post_w_words, post_w_scales, post_b):
    down_w = unpack_weight(down_w_words, down_w_scales, FMT).reshape(G, H, D)
    post_w = unpack_weight(post_w_words, post_w_scales, FMT).reshape(G, D, P)
    x_out = f64(x_mix) + (gmm(f64(ffn_act), down_w) + f64(down_b))
    proj = (gmm(x_out, post_w) + f64(post_b)).reshape(BS, N, Bb, Cc, P)
    k_pre, v_post, k_cand_raw, v_cand = np.split(proj, 4, axis=-1)
    k_cand = unit_normalize(k_pre)
    q_nov = unit_normalize(k_cand_raw)
    return x_out, k_cand, v_post, q_nov, v_cand

@@ -1,0 +1,348 @@
+from contextlib import ExitStack
+
+import concourse.mybir as mybir
+from concourse.masks import make_identity
+
+F32 = mybir.dt.float32
+BF16 = mybir.dt.bfloat16
+U8 = mybir.dt.uint8
+U32 = mybir.dt.uint32
+I32 = mybir.dt.int32
+FP8X4 = mybir.dt.float8_e4m3fn_x4
+ADD = mybir.AluOpType.add
+MULT = mybir.AluOpType.mult
+SQUARE = mybir.ActivationFunctionType.Square
+
+P = 128
+TOKEN_TILES = 2
+GROUPS = 4
+D = 512
+H = 2048
+PACK = 4
+K_PASS = P * PACK
+DOWN_PASSES = H // K_PASS
+STREAMS = 4
+UNITS = GROUPS * TOKEN_TILES
+PAIR = 2
+NORM_FLOOR = 1e-6
+
+FLOPS = 2 * TOKEN_TILES * P * GROUPS * (H * D + D * STREAMS * D)
+
+
+def tile_corticalcolumngroup_pb_e_kernel(
+    tc,
+    ffn_act,
+    x_mix,
+    down_w_words,
+    down_w_scales,
+    down_b,
+    post_w_words,
+    post_w_scales,
+    post_b,
+    out_0,
+    out_1,
+    out_2,
+    out_3,
+    out_4,
+):
+    nc = tc.nc
+    dram_out = [out_0.rearrange("s n (q c) d -> s n q c d", c=PAIR), out_1, out_2, out_3, out_4]
+    down_words_dram = down_w_words.rearrange("c p n t -> c p (n t)").bitcast(I32)
+    post_words_dram = post_w_words.rearrange("g p n t -> g p (n t)").bitcast(I32)
+
+    with ExitStack() as ctx:
+        const = ctx.enter_context(tc.tile_pool(name="const", bufs=1))
+        loads = ctx.enter_context(tc.tile_pool(name="loads", bufs=1))
+        results = ctx.enter_context(tc.tile_pool(name="results", bufs=1))
+        work = ctx.enter_context(tc.tile_pool(name="work", bufs=2))
+        ps_ffn = ctx.enter_context(tc.psum_pool(name="ps_ffn", bufs=2))
+        ps_x = ctx.enter_context(tc.psum_pool(name="ps_x", bufs=1))
+        ps_bias = ctx.enter_context(tc.psum_pool(name="ps_bias", bufs=1))
+        ps_down = ctx.enter_context(tc.psum_pool(name="ps_down", bufs=1))
+        ps_post = ctx.enter_context(tc.psum_pool(name="ps_post", bufs=3))
+        ctx.enter_context(tc.manual_schedule())
+
+        ident_bf = const.tile([P, P], BF16)
+        make_identity(nc, ident_bf[:])
+        ident_f32 = const.tile([P, P], F32)
+        make_identity(nc, ident_f32[:])
+
+        bias_rows = const.tile([P, D], BF16)
+        nc.vector.memset(bias_rows[:].bitcast(I32), 0)
+        down_planes = const.tile([P, GROUPS * D], U8, align_bytes=64)
+        nc.vector.memset(down_planes[:].bitcast(I32), 0)
+        post_planes = const.tile([P, STREAMS * D], U8, align_bytes=64)
+        nc.vector.memset(post_planes[:].bitcast(I32), 0)
+        one = const.tile([P, 1], F32)
+        nc.vector.memset(one[:], 1.0)
+        warm = const.tile([P, 1], F32)
+        nc.scalar.sqrt(out=warm[:], in_=one[:])
+
+        ffn_sb = {}
+        xmix_sb = {}
+        down_sb = {}
+        post_sb = {}
+
+        def load_ffn(unit):
+            g, s = divmod(unit, TOKEN_TILES)
+            ffn_sb[unit] = loads.tile([P, H], BF16, name="ffn%d" % unit)
+            nc.sync.dma_start(out=ffn_sb[unit][:], in_=ffn_act[s, :, g, :])
+
+        def load_xmix(s):
+            xmix_sb[s] = loads.tile([P, GROUPS * D], BF16, name="xmix%d" % s)
+            nc.sync.dma_start(out=xmix_sb[s][:], in_=x_mix[s].rearrange("n g d -> n (g d)"))
+
+        def load_down_scales(g, quadrants):
+            for quad in quadrants:
+                nc.sync.dma_start(
+                    out=down_planes[32 * quad : 32 * quad + 16, g * D : (g + 1) * D].bitcast(I32),
+                    in_=down_w_scales[
+                        DOWN_PASSES * g : DOWN_PASSES * (g + 1), 4 * quad : 4 * quad + 4, :
+                    ].bitcast(I32),
+                )
+
+        def load_down_words(g):
+            down_sb[g] = loads.tile([P, DOWN_PASSES, D], U32, name="down%d" % g, align_bytes=64)
+            nc.sync.dma_start(
+                out=down_sb[g][:].bitcast(I32),
+                in_=down_words_dram[DOWN_PASSES * g : DOWN_PASSES * (g + 1)].rearrange("c p w -> p c w"),
+            )
+
+        def load_post_scales():
+            for quad in range(4):
+                nc.sync.dma_start(
+                    out=post_planes[32 * quad : 32 * quad + 16, :].bitcast(I32),
+                    in_=post_w_scales[:, 4 * quad : 4 * quad + 4, :].bitcast(I32),
+                )
+
+        def load_post_words(g):
+            post_sb[g] = loads.tile([P, STREAMS * D], U32, name="post%d" % g, align_bytes=64)
+            nc.sync.dma_start(out=post_sb[g][:].bitcast(I32), in_=post_words_dram[g])
+
+        load_ffn(0)
+        load_ffn(1)
+        nc.sync.dma_start(out=bias_rows[0:GROUPS, :], in_=down_b)
+        nc.sync.dma_start(
+            out=bias_rows[GROUPS : GROUPS + GROUPS * STREAMS, :],
+            in_=post_b.rearrange("g (j d) -> (g j) d", d=D),
+        )
+        load_down_scales(0, (0, 1))
+        load_down_words(0)
+        load_down_scales(0, (2, 3))
+        load_xmix(0)
+        load_xmix(1)
+        load_post_scales()
+        load_ffn(2)
+        load_post_words(0)
+        for g in range(1, GROUPS):
+            load_ffn(2 * g + 1)
+            load_down_scales(g, (0, 1, 2, 3))
+            load_down_words(g)
+            if g + 1 < GROUPS:
+                load_ffn(2 * g + 2)
+            load_post_words(g)
+
+        result_sb = {}
+        for o in range(1 + STREAMS):
+            for s in range(TOKEN_TILES):
+                for q in range(GROUPS // PAIR):
+                    result_sb[(o, s, q)] = results.tile([P, PAIR, D], F32, name="res%d_%d_%d" % (o, s, q))
+
+        def result(o, unit):
+            g, s = divmod(unit, TOKEN_TILES)
+            return result_sb[(o, s, g // PAIR)][:, g % PAIR, :]
+
+        def store(o, unit):
+            g, s = divmod(unit, TOKEN_TILES)
+            if g % PAIR == PAIR - 1:
+                q = g // PAIR
+                nc.sync.dma_start(out=dram_out[o][s, :, q, :, :], in_=result_sb[(o, s, q)][:])
+
+        def broadcast_two_rows(first_row, dst):
+            bank = ps_bias.tile([P, 2, D], BF16)
+            for i in range(2):
+                row = first_row + i
+                nc.tensor.matmul(
+                    out=bank[:, i, :],
+                    lhsT=ident_bf[:, row : row + 1].to_broadcast([P, P]),
+                    rhs=bias_rows[:],
+                    start=True,
+                    stop=True,
+                )
+            nc.scalar.copy(out=dst, in_=bank[:].rearrange("p i d -> p (i d)"))
+
+        down_bias = const.tile([P, GROUPS * D], BF16)
+        broadcast_two_rows(0, down_bias[:, 0 : 2 * D])
+        broadcast_two_rows(2, down_bias[:, 2 * D : 4 * D])
+
+        post_bias = {}
+
+        def broadcast_post_bias(unit):
+            g, s = divmod(unit, TOKEN_TILES)
+            if s == 0:
+                post_bias[g] = work.tile([P, STREAMS * D], BF16, name="post_bias", tag="post_bias")
+            broadcast_two_rows(
+                GROUPS + STREAMS * g + 2 * s, post_bias[g][:, 2 * s * D : (2 * s + 2) * D]
+            )
+
+        ffn_grouped = {}
+        ffn_codes = {}
+        ffn_scales = {}
+        x_bf = {}
+        x_grouped = {}
+        x_codes = {}
+        x_scales = {}
+        sumsq = {}
+        norm = {}
+        inv_norm = {}
+
+        def residual_plus_bias(unit):
+            g, s = divmod(unit, TOKEN_TILES)
+            cols = slice(g * D, (g + 1) * D)
+            nc.gpsimd.tensor_tensor(
+                out=result(0, unit), in0=xmix_sb[s][:, cols], in1=down_bias[:, cols], op=ADD
+            )
+
+        def transpose_ffn(unit):
+            words = ffn_sb[unit][:].bitcast(F32)
+            ffn_grouped[unit] = work.tile(
+                [P, DOWN_PASSES, P, PACK], BF16, name="ffn_grouped", tag="ffn_grouped", align_bytes=64
+            )
+            for half in range(2):
+                bank = ps_ffn.tile([P, 2, 2, P], F32)
+                for i in range(2):
+                    c = 2 * half + i
+                    for u in range(2):
+                        nc.tensor.transpose(
+                            bank[:, i, u, :], words[:, 256 * c + u : 256 * (c + 1) : 2], ident_f32[:]
+                        )
+                nc.scalar.copy(
+                    out=ffn_grouped[unit][:, 2 * half : 2 * half + 2, :, :].bitcast(F32),
+                    in_=bank[:].rearrange("p c u r -> p c r u"),
+                )
+
+        def quantise_ffn(unit):
+            ffn_codes[unit] = work.tile(
+                [P, DOWN_PASSES * P], U32, name="ffn_codes", tag="ffn_codes", bufs=3, align_bytes=64
+            )
+            ffn_scales[unit] = work.tile(
+                [P, DOWN_PASSES * P], U8, name="ffn_scales", tag="ffn_scales", bufs=3, align_bytes=64
+            )
+            nc.vector.quantize_mx(
+                out=ffn_codes[unit][:].bitcast(FP8X4),
+                scales=ffn_scales[unit][:],
+                in_=ffn_grouped[unit][:].rearrange("p c r t -> p (c r t)"),
+            )
+
+        def down_projection(unit):
+            g, s = divmod(unit, TOKEN_TILES)
+            acc = ps_down.tile([P, D], F32)
+            for c in range(DOWN_PASSES):
+                tokens = slice(c * P, (c + 1) * P)
+                nc.tensor.matmul_mx(
+                    out=acc[:],
+                    lhsT=ffn_codes[unit][:, tokens].bitcast(FP8X4),
+                    lhsT_scale=ffn_scales[unit][:, tokens],
+                    rhs=down_sb[g][:, c, :].bitcast(FP8X4),
+                    rhs_scale=down_planes[4 * c : P, g * D : (g + 1) * D],
+                    start=(c == 0),
+                    stop=(c == DOWN_PASSES - 1),
+                )
+            x_out = result(0, unit)
+            nc.vector.tensor_tensor(out=x_out, in0=acc[:], in1=x_out, op=ADD)
+            store(0, unit)
+            x_bf[unit] = work.tile([P, PACK, P], BF16, name="x_bf", tag="x_bf")
+            nc.gpsimd.tensor_scalar(
+                out=x_bf[unit][:],
+                in0=x_out.rearrange("n (p t) -> n t p", t=PACK),
+                scalar1=1.0,
+                scalar2=0.0,
+                op0=MULT,
+                op1=ADD,
+            )
+
+        def transpose_x(unit):
+            bank = ps_x.tile([P, PACK, P], BF16)
+            for t in range(PACK):
+                nc.tensor.transpose(bank[:, t, :], x_bf[unit][:, t, :], ident_bf[:])
+            x_grouped[unit] = work.tile([P, P, PACK], BF16, name="x_grouped", tag="x_grouped", align_bytes=64)
+            nc.scalar.copy(out=x_grouped[unit][:], in_=bank[:].rearrange("p t r -> p r t"))
+
+        def quantise_x(unit):
+            x_codes[unit] = work.tile([P, P], U32, name="x_codes", tag="x_codes", align_bytes=64)
+            x_scales[unit] = work.tile([P, P], U8, name="x_scales", tag="x_scales", align_bytes=64)
+            nc.vector.quantize_mx(
+                out=x_codes[unit][:].bitcast(FP8X4),
+                scales=x_scales[unit][:],
+                in_=x_grouped[unit][:].rearrange("p r t -> p (r t)"),
+            )
+
+        def post_stream(unit, j):
+            g, s = divmod(unit, TOKEN_TILES)
+            cols = slice(j * D, (j + 1) * D)
+            acc = ps_post.tile([P, D], F32)
+            nc.tensor.matmul_mx(
+                out=acc[:],
+                lhsT=x_codes[unit][:].bitcast(FP8X4),
+                lhsT_scale=x_scales[unit][:],
+                rhs=post_sb[g][:, cols].bitcast(FP8X4),
+                rhs_scale=post_planes[4 * g : P, cols],
+                start=True,
+                stop=True,
+            )
+            nc.vector.tensor_tensor(out=result(1 + j, unit), in0=acc[:], in1=post_bias[g][:, cols], op=ADD)
+
+        def sum_squares(unit, j, column):
+            squares = work.tile([P, D], BF16, name="squares", tag="squares")
+            nc.scalar.activation(
+                out=squares[:], in_=result(1 + j, unit), func=SQUARE, accum_out=sumsq[unit][:, column : column + 1]
+            )
+
+        def scale_stream(unit, j, column):
+            nc.gpsimd.tensor_scalar(
+                out=result(1 + j, unit),
+                in0=result(1 + j, unit),
+                scalar1=inv_norm[unit][:, column : column + 1],
+                scalar2=0.0,
+                op0=MULT,
+                op1=ADD,
+            )
+
+        def live(unit):
+            return 0 <= unit < UNITS
+
+        for n in range(UNITS + 3):
+            if live(n):
+                residual_plus_bias(n)
+                transpose_ffn(n)
+            if live(n - 2):
+                transpose_x(n - 2)
+            if live(n - 1):
+                broadcast_post_bias(n - 1)
+                down_projection(n - 1)
+            last = n - 3
+            if live(last):
+                sumsq[last] = work.tile([P, 2], F32, name="sumsq", tag="sumsq")
+                norm[last] = work.tile([P, 2], F32, name="norm", tag="norm")
+                post_stream(last, 0)
+                sum_squares(last, 0, 0)
+                post_stream(last, 2)
+                sum_squares(last, 2, 1)
+                nc.scalar.sqrt(out=norm[last][:], in_=sumsq[last][:])
+            if live(n):
+                quantise_ffn(n)
+            if live(n - 2):
+                quantise_x(n - 2)
+            if live(last):
+                floored = work.tile([P, 2], F32, name="floored", tag="floored")
+                inv_norm[last] = work.tile([P, 2], F32, name="inv_norm", tag="inv_norm")
+                post_stream(last, 1)
+                store(2, last)
+                nc.vector.tensor_scalar_max(out=floored[:], in0=norm[last][:], scalar1=NORM_FLOOR)
+                post_stream(last, 3)
+                store(4, last)
+                nc.vector.reciprocal(out=inv_norm[last][:], in_=floored[:])
+                scale_stream(last, 0, 0)
+                store(1, last)
+                scale_stream(last, 2, 1)
+                store(3, last)

@@ -57,9 +57,8 @@ def tile_corticalcolumngroup_pb_e_kernel(
         work = ctx.enter_context(tc.tile_pool(name="work", bufs=2))
         ps_ffn = ctx.enter_context(tc.psum_pool(name="ps_ffn", bufs=2))
         ps_x = ctx.enter_context(tc.psum_pool(name="ps_x", bufs=1))
-        ps_bias = ctx.enter_context(tc.psum_pool(name="ps_bias", bufs=1))
         ps_down = ctx.enter_context(tc.psum_pool(name="ps_down", bufs=1))
-        ps_post = ctx.enter_context(tc.psum_pool(name="ps_post", bufs=3))
+        ps_post = ctx.enter_context(tc.psum_pool(name="ps_post", bufs=4))
         ctx.enter_context(tc.manual_schedule())
 
         ident_bf = const.tile([P, P], BF16)
@@ -108,8 +107,8 @@ def tile_corticalcolumngroup_pb_e_kernel(
                 in_=down_words_dram[DOWN_PASSES * g : DOWN_PASSES * (g + 1)].rearrange("c p w -> p c w"),
             )
 
-        def load_post_scales():
-            for quad in range(4):
+        def load_post_scales(quadrants):
+            for quad in quadrants:
                 nc.sync.dma_start(
                     out=post_planes[32 * quad : 32 * quad + 16, :].bitcast(I32),
                     in_=post_w_scales[:, 4 * quad : 4 * quad + 4, :].bitcast(I32),
@@ -120,27 +119,29 @@ def tile_corticalcolumngroup_pb_e_kernel(
             nc.sync.dma_start(out=post_sb[g][:].bitcast(I32), in_=post_words_dram[g])
 
         load_ffn(0)
-        load_ffn(1)
         nc.sync.dma_start(out=bias_rows[0:GROUPS, :], in_=down_b)
         nc.sync.dma_start(
             out=bias_rows[GROUPS : GROUPS + GROUPS * STREAMS, :],
             in_=post_b.rearrange("g (j d) -> (g j) d", d=D),
         )
+        load_ffn(1)
         load_down_scales(0, (0, 1))
         load_down_words(0)
         load_down_scales(0, (2, 3))
         load_xmix(0)
-        load_xmix(1)
-        load_post_scales()
+        load_post_scales((0, 1))
         load_ffn(2)
-        load_post_words(0)
+        load_post_scales((2, 3))
+        load_xmix(1)
         for g in range(1, GROUPS):
+            load_down_scales(g, (0, 1))
             load_ffn(2 * g + 1)
-            load_down_scales(g, (0, 1, 2, 3))
+            load_down_scales(g, (2, 3))
             load_down_words(g)
+            load_post_words(g - 1)
             if g + 1 < GROUPS:
                 load_ffn(2 * g + 2)
-            load_post_words(g)
+        load_post_words(GROUPS - 1)
 
         result_sb = {}
         for o in range(1 + STREAMS):
@@ -159,7 +160,7 @@ def tile_corticalcolumngroup_pb_e_kernel(
                 nc.sync.dma_start(out=dram_out[o][s, :, q, :, :], in_=result_sb[(o, s, q)][:])
 
         def broadcast_two_rows(first_row, dst):
-            bank = ps_bias.tile([P, 2, D], BF16)
+            bank = ps_post.tile([P, 2, D], BF16, name="bias_bank", tag="post")
             for i in range(2):
                 row = first_row + i
                 nc.tensor.matmul(
@@ -172,18 +173,17 @@ def tile_corticalcolumngroup_pb_e_kernel(
             nc.scalar.copy(out=dst, in_=bank[:].rearrange("p i d -> p (i d)"))
 
         down_bias = const.tile([P, GROUPS * D], BF16)
-        broadcast_two_rows(0, down_bias[:, 0 : 2 * D])
-        broadcast_two_rows(2, down_bias[:, 2 * D : 4 * D])
+        post_bias = const.tile([P, GROUPS, STREAMS * D], BF16)
 
-        post_bias = {}
+        def broadcast_down_bias():
+            for half in range(2):
+                broadcast_two_rows(2 * half, down_bias[:, 2 * half * D : (2 * half + 2) * D])
 
-        def broadcast_post_bias(unit):
-            g, s = divmod(unit, TOKEN_TILES)
-            if s == 0:
-                post_bias[g] = work.tile([P, STREAMS * D], BF16, name="post_bias", tag="post_bias")
-            broadcast_two_rows(
-                GROUPS + STREAMS * g + 2 * s, post_bias[g][:, 2 * s * D : (2 * s + 2) * D]
-            )
+        def broadcast_post_bias(g):
+            for half in range(2):
+                broadcast_two_rows(
+                    GROUPS + STREAMS * g + 2 * half, post_bias[:, g, 2 * half * D : (2 * half + 2) * D]
+                )
 
         ffn_grouped = {}
         ffn_codes = {}
@@ -196,11 +196,13 @@ def tile_corticalcolumngroup_pb_e_kernel(
         norm = {}
         inv_norm = {}
 
-        def residual_plus_bias(unit):
-            g, s = divmod(unit, TOKEN_TILES)
-            cols = slice(g * D, (g + 1) * D)
-            nc.gpsimd.tensor_tensor(
-                out=result(0, unit), in0=xmix_sb[s][:, cols], in1=down_bias[:, cols], op=ADD
+        def residual_plus_bias(s, q):
+            cols = slice(q * PAIR * D, (q + 1) * PAIR * D)
+            nc.vector.tensor_tensor(
+                out=result_sb[(0, s, q)][:].rearrange("n c d -> n (c d)"),
+                in0=xmix_sb[s][:, cols],
+                in1=down_bias[:, cols],
+                op=ADD,
             )
 
         def transpose_ffn(unit):
@@ -223,10 +225,10 @@ def tile_corticalcolumngroup_pb_e_kernel(
 
         def quantise_ffn(unit):
             ffn_codes[unit] = work.tile(
-                [P, DOWN_PASSES * P], U32, name="ffn_codes", tag="ffn_codes", bufs=3, align_bytes=64
+                [P, DOWN_PASSES * P], U32, name="ffn_codes", tag="ffn_codes", align_bytes=64
             )
             ffn_scales[unit] = work.tile(
-                [P, DOWN_PASSES * P], U8, name="ffn_scales", tag="ffn_scales", bufs=3, align_bytes=64
+                [P, DOWN_PASSES * P], U8, name="ffn_scales", tag="ffn_scales", align_bytes=64
             )
             nc.vector.quantize_mx(
                 out=ffn_codes[unit][:].bitcast(FP8X4),
@@ -252,14 +254,7 @@ def tile_corticalcolumngroup_pb_e_kernel(
             nc.vector.tensor_tensor(out=x_out, in0=acc[:], in1=x_out, op=ADD)
             store(0, unit)
             x_bf[unit] = work.tile([P, PACK, P], BF16, name="x_bf", tag="x_bf")
-            nc.gpsimd.tensor_scalar(
-                out=x_bf[unit][:],
-                in0=x_out.rearrange("n (p t) -> n t p", t=PACK),
-                scalar1=1.0,
-                scalar2=0.0,
-                op0=MULT,
-                op1=ADD,
-            )
+            nc.scalar.copy(out=x_bf[unit][:], in_=x_out.rearrange("n (p t) -> n t p", t=PACK))
 
         def transpose_x(unit):
             bank = ps_x.tile([P, PACK, P], BF16)
@@ -280,7 +275,7 @@ def tile_corticalcolumngroup_pb_e_kernel(
         def post_stream(unit, j):
             g, s = divmod(unit, TOKEN_TILES)
             cols = slice(j * D, (j + 1) * D)
-            acc = ps_post.tile([P, D], F32)
+            acc = ps_post.tile([P, D], F32, name="post_acc", tag="post")
             nc.tensor.matmul_mx(
                 out=acc[:],
                 lhsT=x_codes[unit][:].bitcast(FP8X4),
@@ -290,7 +285,7 @@ def tile_corticalcolumngroup_pb_e_kernel(
                 start=True,
                 stop=True,
             )
-            nc.vector.tensor_tensor(out=result(1 + j, unit), in0=acc[:], in1=post_bias[g][:, cols], op=ADD)
+            nc.vector.tensor_tensor(out=result(1 + j, unit), in0=acc[:], in1=post_bias[:, g, cols], op=ADD)
 
         def sum_squares(unit, j, column):
             squares = work.tile([P, D], BF16, name="squares", tag="squares")
@@ -313,13 +308,15 @@ def tile_corticalcolumngroup_pb_e_kernel(
 
         for n in range(UNITS + 3):
             if live(n):
-                residual_plus_bias(n)
                 transpose_ffn(n)
+            if n == 0:
+                broadcast_down_bias()
+            if n < GROUPS:
+                broadcast_post_bias(n)
+            if live(n - 1):
+                down_projection(n - 1)
             if live(n - 2):
                 transpose_x(n - 2)
-            if live(n - 1):
-                broadcast_post_bias(n - 1)
-                down_projection(n - 1)
             last = n - 3
             if live(last):
                 sumsq[last] = work.tile([P, 2], F32, name="sumsq", tag="sumsq")
@@ -333,6 +330,8 @@ def tile_corticalcolumngroup_pb_e_kernel(
                 quantise_ffn(n)
             if live(n - 2):
                 quantise_x(n - 2)
+            if n < TOKEN_TILES * (GROUPS // PAIR):
+                residual_plus_bias(n % TOKEN_TILES, n // TOKEN_TILES)
             if live(last):
                 floored = work.tile([P, 2], F32, name="floored", tag="floored")
                 inv_norm[last] = work.tile([P, 2], F32, name="inv_norm", tag="inv_norm")

@@ -93,11 +93,11 @@ def tile_corticalcolumngroup_pb_e_kernel(
 
         def load_down_scales(g, quadrants):
             for quad in quadrants:
-                nc.sync.dma_start(
-                    out=down_planes[32 * quad : 32 * quad + 16, g * D : (g + 1) * D].bitcast(I32),
+                nc.gpsimd.dma_start(
+                    out=down_planes[32 * quad : 32 * quad + 16, g * D : (g + 1) * D].bitcast(F32),
                     in_=down_w_scales[
                         DOWN_PASSES * g : DOWN_PASSES * (g + 1), 4 * quad : 4 * quad + 4, :
-                    ].bitcast(I32),
+                    ].bitcast(F32),
                 )
 
         def load_down_words(g):
@@ -109,9 +109,9 @@ def tile_corticalcolumngroup_pb_e_kernel(
 
         def load_post_scales(quadrants):
             for quad in quadrants:
-                nc.sync.dma_start(
-                    out=post_planes[32 * quad : 32 * quad + 16, :].bitcast(I32),
-                    in_=post_w_scales[:, 4 * quad : 4 * quad + 4, :].bitcast(I32),
+                nc.gpsimd.dma_start(
+                    out=post_planes[32 * quad : 32 * quad + 16, :].bitcast(F32),
+                    in_=post_w_scales[:, 4 * quad : 4 * quad + 4, :].bitcast(F32),
                 )
 
         def load_post_words(g):

@@ -93,11 +93,11 @@ def tile_corticalcolumngroup_pb_e_kernel(
 
         def load_down_scales(g, quadrants):
             for quad in quadrants:
-                nc.gpsimd.dma_start(
-                    out=down_planes[32 * quad : 32 * quad + 16, g * D : (g + 1) * D].bitcast(F32),
+                nc.sync.dma_start(
+                    out=down_planes[32 * quad : 32 * quad + 16, g * D : (g + 1) * D].bitcast(I32),
                     in_=down_w_scales[
                         DOWN_PASSES * g : DOWN_PASSES * (g + 1), 4 * quad : 4 * quad + 4, :
-                    ].bitcast(F32),
+                    ].bitcast(I32),
                 )
 
         def load_down_words(g):
@@ -109,9 +109,9 @@ def tile_corticalcolumngroup_pb_e_kernel(
 
         def load_post_scales(quadrants):
             for quad in quadrants:
-                nc.gpsimd.dma_start(
-                    out=post_planes[32 * quad : 32 * quad + 16, :].bitcast(F32),
-                    in_=post_w_scales[:, 4 * quad : 4 * quad + 4, :].bitcast(F32),
+                nc.sync.dma_start(
+                    out=post_planes[32 * quad : 32 * quad + 16, :].bitcast(I32),
+                    in_=post_w_scales[:, 4 * quad : 4 * quad + 4, :].bitcast(I32),
                 )
 
         def load_post_words(g):
@@ -254,7 +254,9 @@ def tile_corticalcolumngroup_pb_e_kernel(
             nc.vector.tensor_tensor(out=x_out, in0=acc[:], in1=x_out, op=ADD)
             store(0, unit)
             x_bf[unit] = work.tile([P, PACK, P], BF16, name="x_bf", tag="x_bf")
-            nc.scalar.copy(out=x_bf[unit][:], in_=x_out.rearrange("n (p t) -> n t p", t=PACK))
+            nc.scalar.copy(
+                out=x_bf[unit][:].rearrange("n t p -> n p t"), in_=x_out.rearrange("n (p t) -> n p t", t=PACK)
+            )
 
         def transpose_x(unit):
             bank = ps_x.tile([P, PACK, P], BF16)
@@ -306,7 +308,13 @@ def tile_corticalcolumngroup_pb_e_kernel(
         def live(unit):
             return 0 <= unit < UNITS
 
-        for n in range(UNITS + 3):
+        floored = {}
+        for n in range(UNITS + 4):
+            third = n - 3
+            fourth = n - 4
+            if live(fourth):
+                norm[fourth] = work.tile([P, 2], F32, name="norm", tag="norm")
+                nc.scalar.sqrt(out=norm[fourth][:], in_=sumsq[fourth][:])
             if live(n):
                 transpose_ffn(n)
             if n == 0:
@@ -315,33 +323,35 @@ def tile_corticalcolumngroup_pb_e_kernel(
                 broadcast_post_bias(n)
             if live(n - 1):
                 down_projection(n - 1)
+            if live(fourth):
+                floored[fourth] = work.tile([P, 2], F32, name="floored", tag="floored")
+                nc.vector.tensor_scalar_max(out=floored[fourth][:], in0=norm[fourth][:], scalar1=NORM_FLOOR)
             if live(n - 2):
                 transpose_x(n - 2)
-            last = n - 3
-            if live(last):
-                sumsq[last] = work.tile([P, 2], F32, name="sumsq", tag="sumsq")
-                norm[last] = work.tile([P, 2], F32, name="norm", tag="norm")
-                post_stream(last, 0)
-                sum_squares(last, 0, 0)
-                post_stream(last, 2)
-                sum_squares(last, 2, 1)
-                nc.scalar.sqrt(out=norm[last][:], in_=sumsq[last][:])
+            if live(third):
+                sumsq[third] = work.tile([P, 2], F32, name="sumsq", tag="sumsq")
+                post_stream(third, 0)
+                sum_squares(third, 0, 0)
+                post_stream(third, 2)
+                sum_squares(third, 2, 1)
             if live(n):
                 quantise_ffn(n)
             if live(n - 2):
                 quantise_x(n - 2)
-            if n < TOKEN_TILES * (GROUPS // PAIR):
-                residual_plus_bias(n % TOKEN_TILES, n // TOKEN_TILES)
-            if live(last):
-                floored = work.tile([P, 2], F32, name="floored", tag="floored")
-                inv_norm[last] = work.tile([P, 2], F32, name="inv_norm", tag="inv_norm")
-                post_stream(last, 1)
-                store(2, last)
-                nc.vector.tensor_scalar_max(out=floored[:], in0=norm[last][:], scalar1=NORM_FLOOR)
-                post_stream(last, 3)
-                store(4, last)
-                nc.vector.reciprocal(out=inv_norm[last][:], in_=floored[:])
-                scale_stream(last, 0, 0)
-                store(1, last)
-                scale_stream(last, 2, 1)
-                store(3, last)
+            if live(fourth):
+                inv_norm[fourth] = work.tile([P, 2], F32, name="inv_norm", tag="inv_norm")
+                nc.vector.reciprocal(out=inv_norm[fourth][:], in_=floored[fourth][:])
+                scale_stream(fourth, 0, 0)
+                store(1, fourth)
+                scale_stream(fourth, 2, 1)
+                store(3, fourth)
+            if live(third):
+                post_stream(third, 1)
+                store(2, third)
+                post_stream(third, 3)
+                store(4, third)
+            if n < TOKEN_TILES:
+                residual_plus_bias(n, 0)
+            if n == TOKEN_TILES:
+                for s in range(TOKEN_TILES):
+                    residual_plus_bias(s, 1)

@@ -159,7 +159,7 @@ def tile_corticalcolumngroup_pb_e_kernel(
                 q = g // PAIR
                 nc.sync.dma_start(out=dram_out[o][s, :, q, :, :], in_=result_sb[(o, s, q)][:])
 
-        def broadcast_two_rows(first_row, dst):
+        def broadcast_two_rows(first_row, dst, copy):
             bank = ps_post.tile([P, 2, D], BF16, name="bias_bank", tag="post")
             for i in range(2):
                 row = first_row + i
@@ -170,20 +170,19 @@ def tile_corticalcolumngroup_pb_e_kernel(
                     start=True,
                     stop=True,
                 )
-            nc.scalar.copy(out=dst, in_=bank[:].rearrange("p i d -> p (i d)"))
+            copy(out=dst, in_=bank[:].rearrange("p i d -> p (i d)"))
 
         down_bias = const.tile([P, GROUPS * D], BF16)
         post_bias = const.tile([P, GROUPS, STREAMS * D], BF16)
 
         def broadcast_down_bias():
             for half in range(2):
-                broadcast_two_rows(2 * half, down_bias[:, 2 * half * D : (2 * half + 2) * D])
+                broadcast_two_rows(2 * half, down_bias[:, 2 * half * D : (2 * half + 2) * D], nc.vector.tensor_copy)
 
-        def broadcast_post_bias(g):
-            for half in range(2):
-                broadcast_two_rows(
-                    GROUPS + STREAMS * g + 2 * half, post_bias[:, g, 2 * half * D : (2 * half + 2) * D]
-                )
+        def broadcast_post_bias(g, half):
+            broadcast_two_rows(
+                GROUPS + STREAMS * g + 2 * half, post_bias[:, g, 2 * half * D : (2 * half + 2) * D], nc.scalar.copy
+            )
 
         ffn_grouped = {}
         ffn_codes = {}
@@ -253,17 +252,16 @@ def tile_corticalcolumngroup_pb_e_kernel(
             x_out = result(0, unit)
             nc.vector.tensor_tensor(out=x_out, in0=acc[:], in1=x_out, op=ADD)
             store(0, unit)
-            x_bf[unit] = work.tile([P, PACK, P], BF16, name="x_bf", tag="x_bf")
-            nc.scalar.copy(
-                out=x_bf[unit][:].rearrange("n t p -> n p t"), in_=x_out.rearrange("n (p t) -> n p t", t=PACK)
-            )
+            x_bf[unit] = work.tile([P, D], BF16, name="x_bf", tag="x_bf")
+            nc.gpsimd.tensor_scalar(out=x_bf[unit][:], in0=x_out, scalar1=1.0, scalar2=0.0, op0=MULT, op1=ADD)
 
         def transpose_x(unit):
-            bank = ps_x.tile([P, PACK, P], BF16)
-            for t in range(PACK):
-                nc.tensor.transpose(bank[:, t, :], x_bf[unit][:, t, :], ident_bf[:])
+            words = x_bf[unit][:].bitcast(F32)
+            bank = ps_x.tile([P, 2, P], F32)
+            for u in range(2):
+                nc.tensor.transpose(bank[:, u, :], words[:, u : D // 2 : 2], ident_f32[:])
             x_grouped[unit] = work.tile([P, P, PACK], BF16, name="x_grouped", tag="x_grouped", align_bytes=64)
-            nc.scalar.copy(out=x_grouped[unit][:], in_=bank[:].rearrange("p t r -> p r t"))
+            nc.scalar.copy(out=x_grouped[unit][:].bitcast(F32), in_=bank[:].rearrange("p u r -> p r u"))
 
         def quantise_x(unit):
             x_codes[unit] = work.tile([P, P], U32, name="x_codes", tag="x_codes", align_bytes=64)
@@ -319,8 +317,6 @@ def tile_corticalcolumngroup_pb_e_kernel(
                 transpose_ffn(n)
             if n == 0:
                 broadcast_down_bias()
-            if n < GROUPS:
-                broadcast_post_bias(n)
             if live(n - 1):
                 down_projection(n - 1)
             if live(fourth):
@@ -338,6 +334,8 @@ def tile_corticalcolumngroup_pb_e_kernel(
                 quantise_ffn(n)
             if live(n - 2):
                 quantise_x(n - 2)
+            if n < 2 * GROUPS:
+                broadcast_post_bias(n // 2, n % 2)
             if live(fourth):
                 inv_norm[fourth] = work.tile([P, 2], F32, name="inv_norm", tag="inv_norm")
                 nc.vector.reciprocal(out=inv_norm[fourth][:], in_=floored[fourth][:])

@@ -294,6 +294,11 @@ def tile_corticalcolumngroup_pb_e_kernel(
             )
 
         def scale_stream(unit, j, column):
+            if unit >= UNITS - TOKEN_TILES:
+                nc.vector.tensor_scalar_mul(
+                    out=result(1 + j, unit), in0=result(1 + j, unit), scalar1=inv_norm[unit][:, column : column + 1]
+                )
+                return
             nc.gpsimd.tensor_scalar(
                 out=result(1 + j, unit),
                 in0=result(1 + j, unit),

from contextlib import ExitStack

import concourse.mybir as mybir
from concourse.masks import make_identity

F32 = mybir.dt.float32
BF16 = mybir.dt.bfloat16
U8 = mybir.dt.uint8
U32 = mybir.dt.uint32
I32 = mybir.dt.int32
FP8X4 = mybir.dt.float8_e4m3fn_x4
ADD = mybir.AluOpType.add
MULT = mybir.AluOpType.mult
SQUARE = mybir.ActivationFunctionType.Square

P = 128
TOKEN_TILES = 2
GROUPS = 4
D = 512
H = 2048
PACK = 4
K_PASS = P * PACK
DOWN_PASSES = H // K_PASS
STREAMS = 4
UNITS = GROUPS * TOKEN_TILES
PAIR = 2
NORM_FLOOR = 1e-6

FLOPS = 2 * TOKEN_TILES * P * GROUPS * (H * D + D * STREAMS * D)


def tile_corticalcolumngroup_pb_e_kernel(
    tc,
    ffn_act,
    x_mix,
    down_w_words,
    down_w_scales,
    down_b,
    post_w_words,
    post_w_scales,
    post_b,
    out_0,
    out_1,
    out_2,
    out_3,
    out_4,
):
    nc = tc.nc
    dram_out = [out_0.rearrange("s n (q c) d -> s n q c d", c=PAIR), out_1, out_2, out_3, out_4]
    down_words_dram = down_w_words.rearrange("c p n t -> c p (n t)").bitcast(I32)
    post_words_dram = post_w_words.rearrange("g p n t -> g p (n t)").bitcast(I32)

    with ExitStack() as ctx:
        const = ctx.enter_context(tc.tile_pool(name="const", bufs=1))
        loads = ctx.enter_context(tc.tile_pool(name="loads", bufs=1))
        results = ctx.enter_context(tc.tile_pool(name="results", bufs=1))
        work = ctx.enter_context(tc.tile_pool(name="work", bufs=2))
        ps_ffn = ctx.enter_context(tc.psum_pool(name="ps_ffn", bufs=2))
        ps_x = ctx.enter_context(tc.psum_pool(name="ps_x", bufs=1))
        ps_down = ctx.enter_context(tc.psum_pool(name="ps_down", bufs=1))
        ps_post = ctx.enter_context(tc.psum_pool(name="ps_post", bufs=4))
        ctx.enter_context(tc.manual_schedule())

        ident_bf = const.tile([P, P], BF16)
        make_identity(nc, ident_bf[:])
        ident_f32 = const.tile([P, P], F32)
        make_identity(nc, ident_f32[:])

        bias_rows = const.tile([P, D], BF16)
        nc.vector.memset(bias_rows[:].bitcast(I32), 0)
        down_planes = const.tile([P, GROUPS * D], U8, align_bytes=64)
        nc.vector.memset(down_planes[:].bitcast(I32), 0)
        post_planes = const.tile([P, STREAMS * D], U8, align_bytes=64)
        nc.vector.memset(post_planes[:].bitcast(I32), 0)
        one = const.tile([P, 1], F32)
        nc.vector.memset(one[:], 1.0)
        warm = const.tile([P, 1], F32)
        nc.scalar.sqrt(out=warm[:], in_=one[:])

        ffn_sb = {}
        xmix_sb = {}
        down_sb = {}
        post_sb = {}

        def load_ffn(unit):
            g, s = divmod(unit, TOKEN_TILES)
            ffn_sb[unit] = loads.tile([P, H], BF16, name="ffn%d" % unit)
            nc.sync.dma_start(out=ffn_sb[unit][:], in_=ffn_act[s, :, g, :])

        def load_xmix(s):
            xmix_sb[s] = loads.tile([P, GROUPS * D], BF16, name="xmix%d" % s)
            nc.sync.dma_start(out=xmix_sb[s][:], in_=x_mix[s].rearrange("n g d -> n (g d)"))

        def load_down_scales(g, quadrants):
            for quad in quadrants:
                nc.sync.dma_start(
                    out=down_planes[32 * quad : 32 * quad + 16, g * D : (g + 1) * D].bitcast(I32),
                    in_=down_w_scales[
                        DOWN_PASSES * g : DOWN_PASSES * (g + 1), 4 * quad : 4 * quad + 4, :
                    ].bitcast(I32),
                )

        def load_down_words(g):
            down_sb[g] = loads.tile([P, DOWN_PASSES, D], U32, name="down%d" % g, align_bytes=64)
            nc.sync.dma_start(
                out=down_sb[g][:].bitcast(I32),
                in_=down_words_dram[DOWN_PASSES * g : DOWN_PASSES * (g + 1)].rearrange("c p w -> p c w"),
            )

        def load_post_scales(quadrants):
            for quad in quadrants:
                nc.sync.dma_start(
                    out=post_planes[32 * quad : 32 * quad + 16, :].bitcast(I32),
                    in_=post_w_scales[:, 4 * quad : 4 * quad + 4, :].bitcast(I32),
                )

        def load_post_words(g):
            post_sb[g] = loads.tile([P, STREAMS * D], U32, name="post%d" % g, align_bytes=64)
            nc.sync.dma_start(out=post_sb[g][:].bitcast(I32), in_=post_words_dram[g])

        load_ffn(0)
        nc.sync.dma_start(out=bias_rows[0:GROUPS, :], in_=down_b)
        nc.sync.dma_start(
            out=bias_rows[GROUPS : GROUPS + GROUPS * STREAMS, :],
            in_=post_b.rearrange("g (j d) -> (g j) d", d=D),
        )
        load_ffn(1)
        load_down_scales(0, (0, 1))
        load_down_words(0)
        load_down_scales(0, (2, 3))
        load_xmix(0)
        load_post_scales((0, 1))
        load_ffn(2)
        load_post_scales((2, 3))
        load_xmix(1)
        for g in range(1, GROUPS):
            load_down_scales(g, (0, 1))
            load_ffn(2 * g + 1)
            load_down_scales(g, (2, 3))
            load_down_words(g)
            load_post_words(g - 1)
            if g + 1 < GROUPS:
                load_ffn(2 * g + 2)
        load_post_words(GROUPS - 1)

        result_sb = {}
        for o in range(1 + STREAMS):
            for s in range(TOKEN_TILES):
                for q in range(GROUPS // PAIR):
                    result_sb[(o, s, q)] = results.tile([P, PAIR, D], F32, name="res%d_%d_%d" % (o, s, q))

        def result(o, unit):
            g, s = divmod(unit, TOKEN_TILES)
            return result_sb[(o, s, g // PAIR)][:, g % PAIR, :]

        def store(o, unit):
            g, s = divmod(unit, TOKEN_TILES)
            if g % PAIR == PAIR - 1:
                q = g // PAIR
                nc.sync.dma_start(out=dram_out[o][s, :, q, :, :], in_=result_sb[(o, s, q)][:])

        def broadcast_two_rows(first_row, dst, copy):
            bank = ps_post.tile([P, 2, D], BF16, name="bias_bank", tag="post")
            for i in range(2):
                row = first_row + i
                nc.tensor.matmul(
                    out=bank[:, i, :],
                    lhsT=ident_bf[:, row : row + 1].to_broadcast([P, P]),
                    rhs=bias_rows[:],
                    start=True,
                    stop=True,
                )
            copy(out=dst, in_=bank[:].rearrange("p i d -> p (i d)"))

        down_bias = const.tile([P, GROUPS * D], BF16)
        post_bias = const.tile([P, GROUPS, STREAMS * D], BF16)

        def broadcast_down_bias():
            for half in range(2):
                broadcast_two_rows(2 * half, down_bias[:, 2 * half * D : (2 * half + 2) * D], nc.vector.tensor_copy)

        def broadcast_post_bias(g, half):
            broadcast_two_rows(
                GROUPS + STREAMS * g + 2 * half, post_bias[:, g, 2 * half * D : (2 * half + 2) * D], nc.scalar.copy
            )

        ffn_grouped = {}
        ffn_codes = {}
        ffn_scales = {}
        x_bf = {}
        x_grouped = {}
        x_codes = {}
        x_scales = {}
        sumsq = {}
        norm = {}
        inv_norm = {}

        def residual_plus_bias(s, q):
            cols = slice(q * PAIR * D, (q + 1) * PAIR * D)
            nc.vector.tensor_tensor(
                out=result_sb[(0, s, q)][:].rearrange("n c d -> n (c d)"),
                in0=xmix_sb[s][:, cols],
                in1=down_bias[:, cols],
                op=ADD,
            )

        def transpose_ffn(unit):
            words = ffn_sb[unit][:].bitcast(F32)
            ffn_grouped[unit] = work.tile(
                [P, DOWN_PASSES, P, PACK], BF16, name="ffn_grouped", tag="ffn_grouped", align_bytes=64
            )
            for half in range(2):
                bank = ps_ffn.tile([P, 2, 2, P], F32)
                for i in range(2):
                    c = 2 * half + i
                    for u in range(2):
                        nc.tensor.transpose(
                            bank[:, i, u, :], words[:, 256 * c + u : 256 * (c + 1) : 2], ident_f32[:]
                        )
                nc.scalar.copy(
                    out=ffn_grouped[unit][:, 2 * half : 2 * half + 2, :, :].bitcast(F32),
                    in_=bank[:].rearrange("p c u r -> p c r u"),
                )

        def quantise_ffn(unit):
            ffn_codes[unit] = work.tile(
                [P, DOWN_PASSES * P], U32, name="ffn_codes", tag="ffn_codes", align_bytes=64
            )
            ffn_scales[unit] = work.tile(
                [P, DOWN_PASSES * P], U8, name="ffn_scales", tag="ffn_scales", align_bytes=64
            )
            nc.vector.quantize_mx(
                out=ffn_codes[unit][:].bitcast(FP8X4),
                scales=ffn_scales[unit][:],
                in_=ffn_grouped[unit][:].rearrange("p c r t -> p (c r t)"),
            )

        def down_projection(unit):
            g, s = divmod(unit, TOKEN_TILES)
            acc = ps_down.tile([P, D], F32)
            for c in range(DOWN_PASSES):
                tokens = slice(c * P, (c + 1) * P)
                nc.tensor.matmul_mx(
                    out=acc[:],
                    lhsT=ffn_codes[unit][:, tokens].bitcast(FP8X4),
                    lhsT_scale=ffn_scales[unit][:, tokens],
                    rhs=down_sb[g][:, c, :].bitcast(FP8X4),
                    rhs_scale=down_planes[4 * c : P, g * D : (g + 1) * D],
                    start=(c == 0),
                    stop=(c == DOWN_PASSES - 1),
                )
            x_out = result(0, unit)
            nc.vector.tensor_tensor(out=x_out, in0=acc[:], in1=x_out, op=ADD)
            store(0, unit)
            x_bf[unit] = work.tile([P, D], BF16, name="x_bf", tag="x_bf")
            nc.gpsimd.tensor_scalar(out=x_bf[unit][:], in0=x_out, scalar1=1.0, scalar2=0.0, op0=MULT, op1=ADD)

        def transpose_x(unit):
            words = x_bf[unit][:].bitcast(F32)
            bank = ps_x.tile([P, 2, P], F32)
            for u in range(2):
                nc.tensor.transpose(bank[:, u, :], words[:, u : D // 2 : 2], ident_f32[:])
            x_grouped[unit] = work.tile([P, P, PACK], BF16, name="x_grouped", tag="x_grouped", align_bytes=64)
            nc.scalar.copy(out=x_grouped[unit][:].bitcast(F32), in_=bank[:].rearrange("p u r -> p r u"))

        def quantise_x(unit):
            x_codes[unit] = work.tile([P, P], U32, name="x_codes", tag="x_codes", align_bytes=64)
            x_scales[unit] = work.tile([P, P], U8, name="x_scales", tag="x_scales", align_bytes=64)
            nc.vector.quantize_mx(
                out=x_codes[unit][:].bitcast(FP8X4),
                scales=x_scales[unit][:],
                in_=x_grouped[unit][:].rearrange("p r t -> p (r t)"),
            )

        def post_stream(unit, j):
            g, s = divmod(unit, TOKEN_TILES)
            cols = slice(j * D, (j + 1) * D)
            acc = ps_post.tile([P, D], F32, name="post_acc", tag="post")
            nc.tensor.matmul_mx(
                out=acc[:],
                lhsT=x_codes[unit][:].bitcast(FP8X4),
                lhsT_scale=x_scales[unit][:],
                rhs=post_sb[g][:, cols].bitcast(FP8X4),
                rhs_scale=post_planes[4 * g : P, cols],
                start=True,
                stop=True,
            )
            nc.vector.tensor_tensor(out=result(1 + j, unit), in0=acc[:], in1=post_bias[:, g, cols], op=ADD)

        def sum_squares(unit, j, column):
            squares = work.tile([P, D], BF16, name="squares", tag="squares")
            nc.scalar.activation(
                out=squares[:], in_=result(1 + j, unit), func=SQUARE, accum_out=sumsq[unit][:, column : column + 1]
            )

        def scale_stream(unit, j, column):
            if unit >= UNITS - TOKEN_TILES:
                nc.vector.tensor_scalar_mul(
                    out=result(1 + j, unit), in0=result(1 + j, unit), scalar1=inv_norm[unit][:, column : column + 1]
                )
                return
            nc.gpsimd.tensor_scalar(
                out=result(1 + j, unit),
                in0=result(1 + j, unit),
                scalar1=inv_norm[unit][:, column : column + 1],
                scalar2=0.0,
                op0=MULT,
                op1=ADD,
            )

        def live(unit):
            return 0 <= unit < UNITS

        floored = {}
        for n in range(UNITS + 4):
            third = n - 3
            fourth = n - 4
            if live(fourth):
                norm[fourth] = work.tile([P, 2], F32, name="norm", tag="norm")
                nc.scalar.sqrt(out=norm[fourth][:], in_=sumsq[fourth][:])
            if live(n):
                transpose_ffn(n)
            if n == 0:
                broadcast_down_bias()
            if live(n - 1):
                down_projection(n - 1)
            if live(fourth):
                floored[fourth] = work.tile([P, 2], F32, name="floored", tag="floored")
                nc.vector.tensor_scalar_max(out=floored[fourth][:], in0=norm[fourth][:], scalar1=NORM_FLOOR)
            if live(n - 2):
                transpose_x(n - 2)
            if live(third):
                sumsq[third] = work.tile([P, 2], F32, name="sumsq", tag="sumsq")
                post_stream(third, 0)
                sum_squares(third, 0, 0)
                post_stream(third, 2)
                sum_squares(third, 2, 1)
            if live(n):
                quantise_ffn(n)
            if live(n - 2):
                quantise_x(n - 2)
            if n < 2 * GROUPS:
                broadcast_post_bias(n // 2, n % 2)
            if live(fourth):
                inv_norm[fourth] = work.tile([P, 2], F32, name="inv_norm", tag="inv_norm")
                nc.vector.reciprocal(out=inv_norm[fourth][:], in_=floored[fourth][:])
                scale_stream(fourth, 0, 0)
                store(1, fourth)
                scale_stream(fourth, 2, 1)
                store(3, fourth)
            if live(third):
                post_stream(third, 1)
                store(2, third)
                post_stream(third, 3)
                store(4, third)
            if n < TOKEN_TILES:
                residual_plus_bias(n, 0)
            if n == TOKEN_TILES:
                for s in range(TOKEN_TILES):
                    residual_plus_bias(s, 1)
